import numpy as np
import ml_dtypes

BF16 = ml_dtypes.bfloat16


def bf(x):
    return np.asarray(x, np.float32).astype(BF16)


def f32(x):
    return np.asarray(x, np.float32)


def f64(x):
    return np.asarray(x).astype(np.float64)


def striped(idx):
    return np.tile(idx.reshape(-1, 16).T, (8, 1))


B, D, H, C, S, N = 2, 128, 64, 256, 4096, 2048
THETA = 10000.0


def setup_inputs():
    base = f32(np.random.standard_normal((C, S)))
    x = f32(np.random.standard_normal((C, N)))
    pos = np.random.permutation(S)[:N].astype(np.float64)
    inv = THETA ** (-2.0 * np.arange(H) / D)
    ang = inv[:, None] * pos[None, :]
    cosf = f32(np.concatenate([np.cos(ang), np.cos(ang)], axis=0))
    sinf = f32(np.concatenate([-np.sin(ang), np.sin(ang)], axis=0))
    return {"base": base, "x": x, "cosf": cosf, "sinf": sinf, "offs": striped(np.random.permutation(S)[:N])}


def reference(base, x, cosf, sinf, offs):
    idx = offs[:16].T.reshape(-1)
    xb = f64(x).reshape(B, D, N)
    xs = np.concatenate([xb[:, H:], xb[:, :H]], axis=1)
    rotated = xb * f64(cosf)[None] + xs * f64(sinf)[None]
    out = f64(base).copy()
    out[:, idx] = rotated.reshape(C, N)
    return out

@@ -1,0 +1,39 @@
+import concourse.mybir as mybir
+
+F32 = mybir.dt.float32
+U16 = mybir.dt.uint16
+MULT = mybir.AluOpType.mult
+ADD = mybir.AluOpType.add
+
+P = 128
+HALF = 64
+
+
+def tile_myrotarypositionalembedding_s_kernel(tc, base, x, cosf, sinf, offs, out):
+    nc = tc.nc
+    channels, slots = base.shape
+    tokens = x.shape[1]
+    blocks = channels // P
+
+    with tc.tile_pool(name="held", bufs=1) as held:
+        offsets = held.tile([P, tokens // 16], U16, name="offsets")
+        nc.sync.dma_start(offsets[:], offs)
+        cos = held.tile([P, tokens], F32, name="cos")
+        nc.sync.dma_start(cos[:], cosf)
+        sin = held.tile([P, tokens], F32, name="sin")
+        nc.sync.dma_start(sin[:], sinf)
+
+        for b in range(blocks):
+            top = b * P
+            own = held.tile([P, tokens], F32, name=f"own{b}")
+            nc.sync.dma_start(own[:], x[top : top + P, :])
+            partner = held.tile([P, tokens], F32, name=f"partner{b}")
+            nc.sync.dma_start(partner[0:HALF, :], x[top + HALF : top + P, :])
+            nc.sync.dma_start(partner[HALF:P, :], x[top : top + HALF, :])
+            window = held.tile([P, slots], F32, name=f"window{b}")
+            nc.sync.dma_start(window[:], base[top : top + P, :])
+
+            nc.vector.tensor_tensor(own[:], own[:], cos[:], MULT)
+            nc.vector.tensor_tensor(partner[:], partner[:], sin[:], MULT)
+            nc.vector.tensor_tensor(window[:].indirect(offsets[:]), own[:], partner[:], ADD)
+            nc.sync.dma_start(out[top : top + P, :], window[:])

@@ -15,25 +15,32 @@ def tile_myrotarypositionalembedding_s_kernel(tc, base, x, cosf, sinf, offs, out
     tokens = x.shape[1]
     blocks = channels // P
 
+    def move_by_column_halves(dst, src):
+        middle = dst.shape[1] // 2
+        nc.sync.dma_start(dst[:, :middle], src[:, :middle])
+        nc.scalar.dma_start(dst[:, middle:], src[:, middle:])
+
     with tc.tile_pool(name="held", bufs=1) as held:
         offsets = held.tile([P, tokens // 16], U16, name="offsets")
         nc.sync.dma_start(offsets[:], offs)
         cos = held.tile([P, tokens], F32, name="cos")
-        nc.sync.dma_start(cos[:], cosf)
         sin = held.tile([P, tokens], F32, name="sin")
-        nc.sync.dma_start(sin[:], sinf)
 
         for b in range(blocks):
             top = b * P
             own = held.tile([P, tokens], F32, name=f"own{b}")
-            nc.sync.dma_start(own[:], x[top : top + P, :])
+            move_by_column_halves(own, x[top : top + P, :])
+            if b == 0:
+                move_by_column_halves(cos, cosf)
             partner = held.tile([P, tokens], F32, name=f"partner{b}")
             nc.sync.dma_start(partner[0:HALF, :], x[top + HALF : top + P, :])
-            nc.sync.dma_start(partner[HALF:P, :], x[top : top + HALF, :])
+            nc.scalar.dma_start(partner[HALF:P, :], x[top : top + HALF, :])
+            if b == 0:
+                move_by_column_halves(sin, sinf)
             window = held.tile([P, slots], F32, name=f"window{b}")
-            nc.sync.dma_start(window[:], base[top : top + P, :])
+            move_by_column_halves(window, base[top : top + P, :])
 
             nc.vector.tensor_tensor(own[:], own[:], cos[:], MULT)
             nc.vector.tensor_tensor(partner[:], partner[:], sin[:], MULT)
             nc.vector.tensor_tensor(window[:].indirect(offsets[:]), own[:], partner[:], ADD)
-            nc.sync.dma_start(out[top : top + P, :], window[:])
+            move_by_column_halves(out[top : top + P, :], window)

@@ -40,7 +40,8 @@ def tile_myrotarypositionalembedding_s_kernel(tc, base, x, cosf, sinf, offs, out
             window = held.tile([P, slots], F32, name=f"window{b}")
             move_by_column_halves(window, base[top : top + P, :])
 
-            nc.vector.tensor_tensor(own[:], own[:], cos[:], MULT)
-            nc.vector.tensor_tensor(partner[:], partner[:], sin[:], MULT)
+            multiplier = nc.vector if b == 0 else nc.gpsimd
+            multiplier.tensor_tensor(own[:], own[:], cos[:], MULT)
+            multiplier.tensor_tensor(partner[:], partner[:], sin[:], MULT)
             nc.vector.tensor_tensor(window[:].indirect(offsets[:]), own[:], partner[:], ADD)
             move_by_column_halves(out[top : top + P, :], window)

@@ -1,4 +1,5 @@
 import concourse.mybir as mybir
+from concourse.masks import make_identity
 
 F32 = mybir.dt.float32
 U16 = mybir.dt.uint16
@@ -7,6 +8,7 @@ ADD = mybir.AluOpType.add
 
 P = 128
 HALF = 64
+BANK = 512
 
 
 def tile_myrotarypositionalembedding_s_kernel(tc, base, x, cosf, sinf, offs, out):
@@ -14,34 +16,49 @@ def tile_myrotarypositionalembedding_s_kernel(tc, base, x, cosf, sinf, offs, out
     channels, slots = base.shape
     tokens = x.shape[1]
     blocks = channels // P
+    chunks = tokens // BANK
 
     def move_by_column_halves(dst, src):
         middle = dst.shape[1] // 2
         nc.sync.dma_start(dst[:, :middle], src[:, :middle])
         nc.scalar.dma_start(dst[:, middle:], src[:, middle:])
 
-    with tc.tile_pool(name="held", bufs=1) as held:
+    with (
+        tc.tile_pool(name="held", bufs=1) as held,
+        tc.psum_pool(name="psum", bufs=1) as psum,
+    ):
         offsets = held.tile([P, tokens // 16], U16, name="offsets")
         nc.sync.dma_start(offsets[:], offs)
+
+        own = [held.tile([P, tokens], F32, name=f"own{b}") for b in range(blocks)]
+        window = [held.tile([P, slots], F32, name=f"window{b}") for b in range(blocks)]
         cos = held.tile([P, tokens], F32, name="cos")
         sin = held.tile([P, tokens], F32, name="sin")
+        move_by_column_halves(own[0], x[0:P, :])
+        move_by_column_halves(cos, cosf)
+        for b in range(1, blocks):
+            move_by_column_halves(own[b], x[b * P : (b + 1) * P, :])
+        move_by_column_halves(sin, sinf)
+        for b in range(blocks):
+            move_by_column_halves(window[b], base[b * P : (b + 1) * P, :])
+
+        identity = held.tile([P, P], F32, name="identity")
+        make_identity(nc, identity[:])
+        swap = held.tile([P, P], F32, name="swap")
+        nc.vector.tensor_copy(swap[:, 0:HALF], identity[:, HALF:P])
+        nc.vector.tensor_copy(swap[:, HALF:P], identity[:, 0:HALF])
+
+        straight = [held.tile([P, tokens], F32, name=f"straight{b}") for b in range(blocks)]
+        turned = [held.tile([P, tokens], F32, name=f"turned{b}") for b in range(blocks)]
+        for b in range(blocks):
+            nc.vector.tensor_tensor(straight[b][:], own[b][:], cos[:], MULT)
+        for b in range(blocks):
+            for c in range(chunks):
+                columns = slice(c * BANK, (c + 1) * BANK)
+                partner = psum.tile([P, BANK], F32, name=f"partner{b}_{c}")
+                nc.tensor.matmul(partner[:], swap[:], own[b][:, columns], start=True, stop=True)
+                nc.vector.tensor_tensor(turned[b][:, columns], partner[:], sin[:, columns], MULT)
 
         for b in range(blocks):
-            top = b * P
-            own = held.tile([P, tokens], F32, name=f"own{b}")
-            move_by_column_halves(own, x[top : top + P, :])
-            if b == 0:
-                move_by_column_halves(cos, cosf)
-            partner = held.tile([P, tokens], F32, name=f"partner{b}")
-            nc.sync.dma_start(partner[0:HALF, :], x[top + HALF : top + P, :])
-            nc.scalar.dma_start(partner[HALF:P, :], x[top : top + HALF, :])
-            if b == 0:
-                move_by_column_halves(sin, sinf)
-            window = held.tile([P, slots], F32, name=f"window{b}")
-            move_by_column_halves(window, base[top : top + P, :])
-
-            multiplier = nc.vector if b == 0 else nc.gpsimd
-            multiplier.tensor_tensor(own[:], own[:], cos[:], MULT)
-            multiplier.tensor_tensor(partner[:], partner[:], sin[:], MULT)
-            nc.vector.tensor_tensor(window[:].indirect(offsets[:]), own[:], partner[:], ADD)
-            move_by_column_halves(out[top : top + P, :], window)
+            nc.vector.tensor_tensor(window[b][:].indirect(offsets[:]), straight[b][:], turned[b][:], ADD)
+            move_by_column_halves(out[b * P : (b + 1) * P, :], window[b])

@@ -1,10 +1,10 @@
 import concourse.mybir as mybir
-from concourse.masks import make_identity
 
 F32 = mybir.dt.float32
 U16 = mybir.dt.uint16
 MULT = mybir.AluOpType.mult
 ADD = mybir.AluOpType.add
+NOT_EQUAL = mybir.AluOpType.not_equal
 
 P = 128
 HALF = 64
@@ -16,12 +16,13 @@ def tile_myrotarypositionalembedding_s_kernel(tc, base, x, cosf, sinf, offs, out
     channels, slots = base.shape
     tokens = x.shape[1]
     blocks = channels // P
-    chunks = tokens // BANK
+    step = BANK // blocks
+    middle = tokens // 2
 
     def move_by_column_halves(dst, src):
-        middle = dst.shape[1] // 2
-        nc.sync.dma_start(dst[:, :middle], src[:, :middle])
-        nc.scalar.dma_start(dst[:, middle:], src[:, middle:])
+        centre = dst.shape[1] // 2
+        nc.sync.dma_start(dst[:, :centre], src[:, :centre])
+        nc.scalar.dma_start(dst[:, centre:], src[:, centre:])
 
     with (
         tc.tile_pool(name="held", bufs=1) as held,
@@ -30,35 +31,47 @@ def tile_myrotarypositionalembedding_s_kernel(tc, base, x, cosf, sinf, offs, out
         offsets = held.tile([P, tokens // 16], U16, name="offsets")
         nc.sync.dma_start(offsets[:], offs)
 
-        own = [held.tile([P, tokens], F32, name=f"own{b}") for b in range(blocks)]
-        window = [held.tile([P, slots], F32, name=f"window{b}") for b in range(blocks)]
+        own = held.tile([P, blocks, tokens], F32, name="own")
         cos = held.tile([P, tokens], F32, name="cos")
         sin = held.tile([P, tokens], F32, name="sin")
-        move_by_column_halves(own[0], x[0:P, :])
-        move_by_column_halves(cos, cosf)
-        for b in range(1, blocks):
-            move_by_column_halves(own[b], x[b * P : (b + 1) * P, :])
-        move_by_column_halves(sin, sinf)
+        window = [held.tile([P, slots], F32, name=f"window{b}") for b in range(blocks)]
+
+        for left in (0, middle):
+            columns = slice(left, left + middle)
+            for b in range(blocks):
+                queue = nc.sync if b % 2 == 0 else nc.scalar
+                queue.dma_start(own[:, b, columns], x[b * P : (b + 1) * P, columns])
+            nc.sync.dma_start(cos[:, columns], cosf[:, columns])
+            nc.scalar.dma_start(sin[:, columns], sinf[:, columns])
         for b in range(blocks):
             move_by_column_halves(window[b], base[b * P : (b + 1) * P, :])
 
-        identity = held.tile([P, P], F32, name="identity")
-        make_identity(nc, identity[:])
         swap = held.tile([P, P], F32, name="swap")
-        nc.vector.tensor_copy(swap[:, 0:HALF], identity[:, HALF:P])
-        nc.vector.tensor_copy(swap[:, HALF:P], identity[:, 0:HALF])
+        nc.gpsimd.memset(swap[:], 0.0)
+        for shift in (HALF, -HALF):
+            nc.gpsimd.affine_select(
+                out=swap[:],
+                in_=swap[:],
+                pattern=[[-1, P]],
+                compare_op=NOT_EQUAL,
+                fill=1.0,
+                base=shift,
+                channel_multiplier=1,
+            )
 
-        straight = [held.tile([P, tokens], F32, name=f"straight{b}") for b in range(blocks)]
-        turned = [held.tile([P, tokens], F32, name=f"turned{b}") for b in range(blocks)]
-        for b in range(blocks):
-            nc.vector.tensor_tensor(straight[b][:], own[b][:], cos[:], MULT)
-        for b in range(blocks):
-            for c in range(chunks):
-                columns = slice(c * BANK, (c + 1) * BANK)
-                partner = psum.tile([P, BANK], F32, name=f"partner{b}_{c}")
-                nc.tensor.matmul(partner[:], swap[:], own[b][:, columns], start=True, stop=True)
-                nc.vector.tensor_tensor(turned[b][:, columns], partner[:], sin[:, columns], MULT)
+        straight = held.tile([P, blocks, tokens], F32, name="straight")
+        turned = held.tile([P, blocks, tokens], F32, name="turned")
+        for left in (0, middle):
+            columns = slice(left, left + middle)
+            cos_for_all = cos[:, columns].unsqueeze(1).to_broadcast([P, blocks, middle])
+            nc.vector.tensor_tensor(straight[:, :, columns], own[:, :, columns], cos_for_all, MULT)
+            for first in range(left, left + middle, step):
+                piece = slice(first, first + step)
+                partner = psum.tile([P, blocks, step], F32, name=f"partner{first}")
+                nc.tensor.matmul(partner[:], swap[:], own[:, :, piece], start=True, stop=True)
+                sin_for_all = sin[:, piece].unsqueeze(1).to_broadcast([P, blocks, step])
+                nc.vector.tensor_tensor(turned[:, :, piece], partner[:], sin_for_all, MULT)
 
         for b in range(blocks):
-            nc.vector.tensor_tensor(window[b][:].indirect(offsets[:]), straight[b][:], turned[b][:], ADD)
+            nc.vector.tensor_tensor(window[b][:].indirect(offsets[:]), straight[:, b, :], turned[:, b, :], ADD)
             move_by_column_halves(out[b * P : (b + 1) * P, :], window[b])

@@ -17,34 +17,26 @@ def tile_myrotarypositionalembedding_s_kernel(tc, base, x, cosf, sinf, offs, out
     tokens = x.shape[1]
     blocks = channels // P
     step = BANK // blocks
-    middle = tokens // 2
-
-    def move_by_column_halves(dst, src):
-        centre = dst.shape[1] // 2
-        nc.sync.dma_start(dst[:, :centre], src[:, :centre])
-        nc.scalar.dma_start(dst[:, centre:], src[:, centre:])
+    token_halves = (slice(0, tokens // 2), slice(tokens // 2, tokens))
+    x_by_block = x.rearrange("(b p) t -> p b t", p=P)
 
     with (
         tc.tile_pool(name="held", bufs=1) as held,
         tc.psum_pool(name="psum", bufs=1) as psum,
     ):
-        offsets = held.tile([P, tokens // 16], U16, name="offsets")
-        nc.sync.dma_start(offsets[:], offs)
-
         own = held.tile([P, blocks, tokens], F32, name="own")
         cos = held.tile([P, tokens], F32, name="cos")
         sin = held.tile([P, tokens], F32, name="sin")
+        offsets = held.tile([P, tokens // 16], U16, name="offsets")
         window = [held.tile([P, slots], F32, name=f"window{b}") for b in range(blocks)]
 
-        for left in (0, middle):
-            columns = slice(left, left + middle)
-            for b in range(blocks):
-                queue = nc.sync if b % 2 == 0 else nc.scalar
-                queue.dma_start(own[:, b, columns], x[b * P : (b + 1) * P, columns])
+        for columns in token_halves:
+            nc.sync.dma_start(own[:, :, columns], x_by_block[:, :, columns])
             nc.sync.dma_start(cos[:, columns], cosf[:, columns])
-            nc.scalar.dma_start(sin[:, columns], sinf[:, columns])
+        nc.sync.dma_start(sin[:], sinf)
+        nc.sync.dma_start(offsets[:], offs)
         for b in range(blocks):
-            move_by_column_halves(window[b], base[b * P : (b + 1) * P, :])
+            nc.sync.dma_start(window[b][:], base[b * P : (b + 1) * P, :])
 
         swap = held.tile([P, P], F32, name="swap")
         nc.gpsimd.memset(swap[:], 0.0)
@@ -60,18 +52,17 @@ def tile_myrotarypositionalembedding_s_kernel(tc, base, x, cosf, sinf, offs, out
             )
 
         straight = held.tile([P, blocks, tokens], F32, name="straight")
-        turned = held.tile([P, blocks, tokens], F32, name="turned")
-        for left in (0, middle):
-            columns = slice(left, left + middle)
-            cos_for_all = cos[:, columns].unsqueeze(1).to_broadcast([P, blocks, middle])
+        for columns in token_halves:
+            cos_for_all = cos[:, columns].unsqueeze(1).to_broadcast([P, blocks, tokens // 2])
             nc.vector.tensor_tensor(straight[:, :, columns], own[:, :, columns], cos_for_all, MULT)
-            for first in range(left, left + middle, step):
-                piece = slice(first, first + step)
-                partner = psum.tile([P, blocks, step], F32, name=f"partner{first}")
-                nc.tensor.matmul(partner[:], swap[:], own[:, :, piece], start=True, stop=True)
-                sin_for_all = sin[:, piece].unsqueeze(1).to_broadcast([P, blocks, step])
-                nc.vector.tensor_tensor(turned[:, :, piece], partner[:], sin_for_all, MULT)
+        turned = held.tile([P, blocks, tokens], F32, name="turned")
+        for first in range(0, tokens, step):
+            piece = slice(first, first + step)
+            partner = psum.tile([P, blocks, step], F32, name=f"partner{first}")
+            nc.tensor.matmul(partner[:], swap[:], own[:, :, piece], start=True, stop=True)
+            sin_for_all = sin[:, piece].unsqueeze(1).to_broadcast([P, blocks, step])
+            nc.vector.tensor_tensor(turned[:, :, piece], partner[:], sin_for_all, MULT)
 
         for b in range(blocks):
             nc.vector.tensor_tensor(window[b][:].indirect(offsets[:]), straight[:, b, :], turned[:, b, :], ADD)
-            move_by_column_halves(out[b * P : (b + 1) * P, :], window[b])
+            nc.sync.dma_start(out[b * P : (b + 1) * P, :], window[b][:])

@@ -4,65 +4,55 @@ F32 = mybir.dt.float32
 U16 = mybir.dt.uint16
 MULT = mybir.AluOpType.mult
 ADD = mybir.AluOpType.add
-NOT_EQUAL = mybir.AluOpType.not_equal
 
 P = 128
-HALF = 64
-BANK = 512
+PAIRS = 64
+SEQUENCES = 2
+MEMBERS = 2
 
 
 def tile_myrotarypositionalembedding_s_kernel(tc, base, x, cosf, sinf, offs, out):
     nc = tc.nc
-    channels, slots = base.shape
+    slots = base.shape[1]
     tokens = x.shape[1]
-    blocks = channels // P
-    step = BANK // blocks
     token_halves = (slice(0, tokens // 2), slice(tokens // 2, tokens))
-    x_by_block = x.rearrange("(b p) t -> p b t", p=P)
+    x_rows = x.rearrange("(b h k) t -> k b h t", b=SEQUENCES, h=MEMBERS)
+    base_rows = base.rearrange("(b h k) s -> k b h s", b=SEQUENCES, h=MEMBERS)
+    out_rows = out.rearrange("(b h k) s -> k b h s", b=SEQUENCES, h=MEMBERS)
 
-    with (
-        tc.tile_pool(name="held", bufs=1) as held,
-        tc.psum_pool(name="psum", bufs=1) as psum,
-    ):
-        own = held.tile([P, blocks, tokens], F32, name="own")
+    with tc.tile_pool(name="held", bufs=1) as held:
+        own = held.tile([P, MEMBERS, tokens], F32, name="own")
         cos = held.tile([P, tokens], F32, name="cos")
         sin = held.tile([P, tokens], F32, name="sin")
         offsets = held.tile([P, tokens // 16], U16, name="offsets")
-        window = [held.tile([P, slots], F32, name=f"window{b}") for b in range(blocks)]
+        window = [held.tile([P, slots], F32, name=f"window{h}") for h in range(MEMBERS)]
+
+        own_rows = own[:].rearrange("(k b) h t -> k b h t", b=SEQUENCES)
+        cos_rows = cos[:].rearrange("(k b) t -> k b t", b=SEQUENCES)
+        sin_rows = sin[:].rearrange("(k b) t -> k b t", b=SEQUENCES)
+        window_rows = [window[h][:].rearrange("(k b) s -> k b s", b=SEQUENCES) for h in range(MEMBERS)]
 
         for columns in token_halves:
-            nc.sync.dma_start(own[:, :, columns], x_by_block[:, :, columns])
-            nc.sync.dma_start(cos[:, columns], cosf[:, columns])
-        nc.sync.dma_start(sin[:], sinf)
+            for b in range(SEQUENCES):
+                nc.sync.dma_start(own_rows[:, b, :, columns], x_rows[:, b, :, columns])
+            for b in range(SEQUENCES):
+                nc.sync.dma_start(cos_rows[:, b, columns], cosf[0:PAIRS, columns])
+            for b in range(SEQUENCES):
+                nc.sync.dma_start(sin_rows[:, b, columns], sinf[0:PAIRS, columns])
         nc.sync.dma_start(offsets[:], offs)
-        for b in range(blocks):
-            nc.sync.dma_start(window[b][:], base[b * P : (b + 1) * P, :])
+        for h in range(MEMBERS):
+            for b in range(SEQUENCES):
+                nc.sync.dma_start(window_rows[h][:, b, :], base_rows[:, b, h, :])
 
-        swap = held.tile([P, P], F32, name="swap")
-        nc.gpsimd.memset(swap[:], 0.0)
-        for shift in (HALF, -HALF):
-            nc.gpsimd.affine_select(
-                out=swap[:],
-                in_=swap[:],
-                pattern=[[-1, P]],
-                compare_op=NOT_EQUAL,
-                fill=1.0,
-                base=shift,
-                channel_multiplier=1,
-            )
-
-        straight = held.tile([P, blocks, tokens], F32, name="straight")
+        straight = held.tile([P, MEMBERS, tokens], F32, name="straight")
+        cross = held.tile([P, MEMBERS, tokens], F32, name="cross")
         for columns in token_halves:
-            cos_for_all = cos[:, columns].unsqueeze(1).to_broadcast([P, blocks, tokens // 2])
-            nc.vector.tensor_tensor(straight[:, :, columns], own[:, :, columns], cos_for_all, MULT)
-        turned = held.tile([P, blocks, tokens], F32, name="turned")
-        for first in range(0, tokens, step):
-            piece = slice(first, first + step)
-            partner = psum.tile([P, blocks, step], F32, name=f"partner{first}")
-            nc.tensor.matmul(partner[:], swap[:], own[:, :, piece], start=True, stop=True)
-            sin_for_all = sin[:, piece].unsqueeze(1).to_broadcast([P, blocks, step])
-            nc.vector.tensor_tensor(turned[:, :, piece], partner[:], sin_for_all, MULT)
+            cos_for_both = cos[:, columns].unsqueeze(1).to_broadcast([P, MEMBERS, tokens // 2])
+            nc.vector.tensor_tensor(straight[:, :, columns], own[:, :, columns], cos_for_both, MULT)
+            nc.vector.tensor_tensor(cross[:, 0, columns], own[:, 1, columns], sin[:, columns], MULT)
+            nc.vector.scalar_tensor_tensor(cross[:, 1, columns], own[:, 0, columns], -1.0, sin[:, columns], MULT, MULT)
 
-        for b in range(blocks):
-            nc.vector.tensor_tensor(window[b][:].indirect(offsets[:]), straight[:, b, :], turned[:, b, :], ADD)
-            nc.sync.dma_start(out[b * P : (b + 1) * P, :], window[b][:])
+        for h in range(MEMBERS):
+            nc.vector.tensor_tensor(window[h][:].indirect(offsets[:]), straight[:, h, :], cross[:, h, :], ADD)
+            for b in range(SEQUENCES):
+                nc.sync.dma_start(out_rows[:, b, h, :], window_rows[h][:, b, :])

@@ -4,55 +4,78 @@ F32 = mybir.dt.float32
 U16 = mybir.dt.uint16
 MULT = mybir.AluOpType.mult
 ADD = mybir.AluOpType.add
+NOT_EQUAL = mybir.AluOpType.not_equal
+X_AXIS = mybir.AxisListType.X
 
 P = 128
 PAIRS = 64
 SEQUENCES = 2
 MEMBERS = 2
+BANK = 512
 
 
 def tile_myrotarypositionalembedding_s_kernel(tc, base, x, cosf, sinf, offs, out):
     nc = tc.nc
     slots = base.shape[1]
     tokens = x.shape[1]
-    token_halves = (slice(0, tokens // 2), slice(tokens // 2, tokens))
+    pieces = [slice(first, first + BANK) for first in range(0, tokens, BANK)]
     x_rows = x.rearrange("(b h k) t -> k b h t", b=SEQUENCES, h=MEMBERS)
     base_rows = base.rearrange("(b h k) s -> k b h s", b=SEQUENCES, h=MEMBERS)
     out_rows = out.rearrange("(b h k) s -> k b h s", b=SEQUENCES, h=MEMBERS)
 
-    with tc.tile_pool(name="held", bufs=1) as held:
+    with (
+        tc.tile_pool(name="held", bufs=1) as held,
+        tc.psum_pool(name="psum", bufs=1) as psum,
+    ):
         own = held.tile([P, MEMBERS, tokens], F32, name="own")
-        cos = held.tile([P, tokens], F32, name="cos")
-        sin = held.tile([P, tokens], F32, name="sin")
+        trig = held.tile([P, tokens], F32, name="trig")
         offsets = held.tile([P, tokens // 16], U16, name="offsets")
-        window = [held.tile([P, slots], F32, name=f"window{h}") for h in range(MEMBERS)]
+        window = [held.tile([P, slots], F32, name=f"window{w}") for w in range(2)]
 
         own_rows = own[:].rearrange("(k b) h t -> k b h t", b=SEQUENCES)
-        cos_rows = cos[:].rearrange("(k b) t -> k b t", b=SEQUENCES)
-        sin_rows = sin[:].rearrange("(k b) t -> k b t", b=SEQUENCES)
-        window_rows = [window[h][:].rearrange("(k b) s -> k b s", b=SEQUENCES) for h in range(MEMBERS)]
+        trig_rows = trig[:].rearrange("(k b) t -> k b t", b=SEQUENCES)
+        window_rows = [window[w][:].rearrange("(k b) s -> k b s", b=SEQUENCES) for w in range(2)]
 
-        for columns in token_halves:
+        for piece in pieces:
+            nc.sync.dma_start(trig_rows[:, 0, piece], cosf[0:PAIRS, piece])
+            nc.sync.dma_start(trig_rows[:, 1, piece], sinf[PAIRS:P, piece])
             for b in range(SEQUENCES):
-                nc.sync.dma_start(own_rows[:, b, :, columns], x_rows[:, b, :, columns])
-            for b in range(SEQUENCES):
-                nc.sync.dma_start(cos_rows[:, b, columns], cosf[0:PAIRS, columns])
-            for b in range(SEQUENCES):
-                nc.sync.dma_start(sin_rows[:, b, columns], sinf[0:PAIRS, columns])
+                nc.sync.dma_start(own_rows[:, b, :, piece], x_rows[:, b, :, piece])
         nc.sync.dma_start(offsets[:], offs)
-        for h in range(MEMBERS):
+        for w in range(2):
             for b in range(SEQUENCES):
-                nc.sync.dma_start(window_rows[h][:, b, :], base_rows[:, b, h, :])
+                nc.sync.dma_start(window_rows[w][:, b, :], base_rows[:, b, (b + w) % MEMBERS, :])
 
-        straight = held.tile([P, MEMBERS, tokens], F32, name="straight")
-        cross = held.tile([P, MEMBERS, tokens], F32, name="cross")
-        for columns in token_halves:
-            cos_for_both = cos[:, columns].unsqueeze(1).to_broadcast([P, MEMBERS, tokens // 2])
-            nc.vector.tensor_tensor(straight[:, :, columns], own[:, :, columns], cos_for_both, MULT)
-            nc.vector.tensor_tensor(cross[:, 0, columns], own[:, 1, columns], sin[:, columns], MULT)
-            nc.vector.scalar_tensor_tensor(cross[:, 1, columns], own[:, 0, columns], -1.0, sin[:, columns], MULT, MULT)
+        turn = held.tile([P, PAIRS, SEQUENCES], F32, name="turn")
+        nc.gpsimd.memset(turn[:], 0.0)
+        nc.gpsimd.affine_select(
+            out=turn[:], in_=turn[:], pattern=[[-2, PAIRS], [-P, SEQUENCES]],
+            compare_op=NOT_EQUAL, fill=1.0, base=P, channel_multiplier=1,
+        )
+        nc.gpsimd.affine_select(
+            out=turn[:], in_=turn[:], pattern=[[-2, PAIRS], [P, SEQUENCES]],
+            compare_op=NOT_EQUAL, fill=-1.0, base=-1, channel_multiplier=1,
+        )
+        turn_matrix = turn[:].rearrange("p k b -> p (k b)")
+        sign = held.tile([P, 2], F32, name="sign")
+        nc.vector.reduce_sum(sign[:, 0:1], turn_matrix, axis=X_AXIS)
+        nc.vector.tensor_scalar_mul(sign[:, 1:2], sign[:, 0:1], -1.0)
 
-        for h in range(MEMBERS):
-            nc.vector.tensor_tensor(window[h][:].indirect(offsets[:]), straight[:, h, :], cross[:, h, :], ADD)
+        with_trig = held.tile([P, 2, tokens], F32, name="with_trig")
+        with_other = held.tile([P, 2, tokens], F32, name="with_other")
+        for number, piece in enumerate(pieces):
+            other = psum.tile([P, BANK], F32, name=f"other{number}")
+            nc.tensor.matmul(other[:], turn_matrix, trig[:, piece], start=True, stop=True)
+            nc.vector.tensor_tensor(with_trig[:, 0, piece], own[:, 0, piece], trig[:, piece], MULT)
+            nc.vector.scalar_tensor_tensor(
+                with_trig[:, 1, piece], own[:, 1, piece], sign[:, 0:1], trig[:, piece], MULT, MULT
+            )
+            nc.vector.tensor_tensor(with_other[:, 0, piece], own[:, 1, piece], other[:], MULT)
+            nc.vector.scalar_tensor_tensor(
+                with_other[:, 1, piece], own[:, 0, piece], sign[:, 1:2], other[:], MULT, MULT
+            )
+
+        for w in range(2):
+            nc.vector.tensor_tensor(window[w][:].indirect(offsets[:]), with_trig[:, w, :], with_other[:, w, :], ADD)
             for b in range(SEQUENCES):
-                nc.sync.dma_start(out_rows[:, b, h, :], window_rows[h][:, b, :])
+                nc.sync.dma_start(out_rows[:, b, (b + w) % MEMBERS, :], window_rows[w][:, b, :])

@@ -19,6 +19,7 @@ def tile_myrotarypositionalembedding_s_kernel(tc, base, x, cosf, sinf, offs, out
     slots = base.shape[1]
     tokens = x.shape[1]
     pieces = [slice(first, first + BANK) for first in range(0, tokens, BANK)]
+    chunks = (slice(0, tokens // 4), slice(tokens // 4, tokens // 2), slice(tokens // 2, tokens))
     x_rows = x.rearrange("(b h k) t -> k b h t", b=SEQUENCES, h=MEMBERS)
     base_rows = base.rearrange("(b h k) s -> k b h s", b=SEQUENCES, h=MEMBERS)
     out_rows = out.rearrange("(b h k) s -> k b h s", b=SEQUENCES, h=MEMBERS)
@@ -36,11 +37,11 @@ def tile_myrotarypositionalembedding_s_kernel(tc, base, x, cosf, sinf, offs, out
         trig_rows = trig[:].rearrange("(k b) t -> k b t", b=SEQUENCES)
         window_rows = [window[w][:].rearrange("(k b) s -> k b s", b=SEQUENCES) for w in range(2)]
 
-        for piece in pieces:
-            nc.sync.dma_start(trig_rows[:, 0, piece], cosf[0:PAIRS, piece])
-            nc.sync.dma_start(trig_rows[:, 1, piece], sinf[PAIRS:P, piece])
+        for chunk in chunks:
+            nc.sync.dma_start(trig_rows[:, 0, chunk], cosf[0:PAIRS, chunk])
+            nc.sync.dma_start(trig_rows[:, 1, chunk], sinf[PAIRS:P, chunk])
             for b in range(SEQUENCES):
-                nc.sync.dma_start(own_rows[:, b, :, piece], x_rows[:, b, :, piece])
+                nc.sync.dma_start(own_rows[:, b, :, chunk], x_rows[:, b, :, chunk])
         nc.sync.dma_start(offsets[:], offs)
         for w in range(2):
             for b in range(SEQUENCES):

@@ -18,8 +18,7 @@ def tile_myrotarypositionalembedding_s_kernel(tc, base, x, cosf, sinf, offs, out
     nc = tc.nc
     slots = base.shape[1]
     tokens = x.shape[1]
-    pieces = [slice(first, first + BANK) for first in range(0, tokens, BANK)]
-    chunks = (slice(0, tokens // 4), slice(tokens // 4, tokens // 2), slice(tokens // 2, tokens))
+    token_halves = (slice(0, tokens // 2), slice(tokens // 2, tokens))
     x_rows = x.rearrange("(b h k) t -> k b h t", b=SEQUENCES, h=MEMBERS)
     base_rows = base.rearrange("(b h k) s -> k b h s", b=SEQUENCES, h=MEMBERS)
     out_rows = out.rearrange("(b h k) s -> k b h s", b=SEQUENCES, h=MEMBERS)
@@ -37,11 +36,12 @@ def tile_myrotarypositionalembedding_s_kernel(tc, base, x, cosf, sinf, offs, out
         trig_rows = trig[:].rearrange("(k b) t -> k b t", b=SEQUENCES)
         window_rows = [window[w][:].rearrange("(k b) s -> k b s", b=SEQUENCES) for w in range(2)]
 
-        for chunk in chunks:
-            nc.sync.dma_start(trig_rows[:, 0, chunk], cosf[0:PAIRS, chunk])
-            nc.sync.dma_start(trig_rows[:, 1, chunk], sinf[PAIRS:P, chunk])
-            for b in range(SEQUENCES):
-                nc.sync.dma_start(own_rows[:, b, :, chunk], x_rows[:, b, :, chunk])
+        for half in token_halves:
+            nc.sync.dma_start(trig_rows[:, 0, half], cosf[0:PAIRS, half])
+            nc.sync.dma_start(trig_rows[:, 1, half], sinf[PAIRS:P, half])
+            for h in range(MEMBERS):
+                for b in range(SEQUENCES):
+                    nc.sync.dma_start(own_rows[:, b, h, half], x_rows[:, b, h, half])
         nc.sync.dma_start(offsets[:], offs)
         for w in range(2):
             for b in range(SEQUENCES):
@@ -64,17 +64,20 @@ def tile_myrotarypositionalembedding_s_kernel(tc, base, x, cosf, sinf, offs, out
 
         with_trig = held.tile([P, 2, tokens], F32, name="with_trig")
         with_other = held.tile([P, 2, tokens], F32, name="with_other")
-        for number, piece in enumerate(pieces):
-            other = psum.tile([P, BANK], F32, name=f"other{number}")
-            nc.tensor.matmul(other[:], turn_matrix, trig[:, piece], start=True, stop=True)
-            nc.vector.tensor_tensor(with_trig[:, 0, piece], own[:, 0, piece], trig[:, piece], MULT)
+        engine_of_half = (nc.vector, nc.gpsimd)
+        for number, half in enumerate(token_halves):
+            engine_of_half[number].tensor_tensor(with_trig[:, 0, half], own[:, 0, half], trig[:, half], MULT)
             nc.vector.scalar_tensor_tensor(
-                with_trig[:, 1, piece], own[:, 1, piece], sign[:, 0:1], trig[:, piece], MULT, MULT
+                with_trig[:, 1, half], own[:, 1, half], sign[:, 0:1], trig[:, half], MULT, MULT
             )
-            nc.vector.tensor_tensor(with_other[:, 0, piece], own[:, 1, piece], other[:], MULT)
-            nc.vector.scalar_tensor_tensor(
-                with_other[:, 1, piece], own[:, 0, piece], sign[:, 1:2], other[:], MULT, MULT
-            )
+            for first in range(half.start, half.stop, BANK):
+                piece = slice(first, first + BANK)
+                other = psum.tile([P, BANK], F32, name=f"other{first}")
+                nc.tensor.matmul(other[:], turn_matrix, trig[:, piece], start=True, stop=True)
+                nc.vector.scalar_tensor_tensor(
+                    with_other[:, 1, piece], own[:, 0, piece], sign[:, 1:2], other[:], MULT, MULT
+                )
+                nc.vector.tensor_tensor(with_other[:, 0, piece], own[:, 1, piece], other[:], MULT)
 
         for w in range(2):
             nc.vector.tensor_tensor(window[w][:].indirect(offsets[:]), with_trig[:, w, :], with_other[:, w, :], ADD)

@@ -47,23 +47,21 @@ def tile_myrotarypositionalembedding_s_kernel(tc, base, x, cosf, sinf, offs, out
             for b in range(SEQUENCES):
                 nc.sync.dma_start(window_rows[w][:, b, :], base_rows[:, b, (b + w) % MEMBERS, :])
 
-        turn = held.tile([P, PAIRS, SEQUENCES], F32, name="turn")
-        nc.gpsimd.memset(turn[:], 0.0)
+        swap = held.tile([P, PAIRS, SEQUENCES], F32, name="swap")
+        nc.vector.memset(swap[:], 0.0)
         nc.gpsimd.affine_select(
-            out=turn[:], in_=turn[:], pattern=[[-2, PAIRS], [-P, SEQUENCES]],
-            compare_op=NOT_EQUAL, fill=1.0, base=P, channel_multiplier=1,
+            out=swap[:], in_=swap[:], pattern=[[-2, PAIRS], [1, SEQUENCES]],
+            compare_op=NOT_EQUAL, fill=1.0, base=-1, channel_multiplier=1,
         )
-        nc.gpsimd.affine_select(
-            out=turn[:], in_=turn[:], pattern=[[-2, PAIRS], [P, SEQUENCES]],
-            compare_op=NOT_EQUAL, fill=-1.0, base=-1, channel_multiplier=1,
-        )
-        turn_matrix = turn[:].rearrange("p k b -> p (k b)")
+        swap_matrix = swap[:].rearrange("p k b -> p (k b)")
+        is_odd = held.tile([P, 1], F32, name="is_odd")
         sign = held.tile([P, 2], F32, name="sign")
-        nc.vector.reduce_sum(sign[:, 0:1], turn_matrix, axis=X_AXIS)
-        nc.vector.tensor_scalar_mul(sign[:, 1:2], sign[:, 0:1], -1.0)
+        nc.vector.reduce_sum(is_odd[:], swap[:, :, 0], axis=X_AXIS)
+        nc.vector.tensor_scalar(sign[:, 0:1], is_odd[:], -2.0, 1.0, MULT, ADD)
+        nc.vector.tensor_scalar(sign[:, 1:2], is_odd[:], 2.0, -1.0, MULT, ADD)
 
         with_trig = held.tile([P, 2, tokens], F32, name="with_trig")
-        with_other = held.tile([P, 2, tokens], F32, name="with_other")
+        with_swapped = held.tile([P, 2, tokens], F32, name="with_swapped")
         engine_of_half = (nc.vector, nc.gpsimd)
         for number, half in enumerate(token_halves):
             engine_of_half[number].tensor_tensor(with_trig[:, 0, half], own[:, 0, half], trig[:, half], MULT)
@@ -72,14 +70,14 @@ def tile_myrotarypositionalembedding_s_kernel(tc, base, x, cosf, sinf, offs, out
             )
             for first in range(half.start, half.stop, BANK):
                 piece = slice(first, first + BANK)
-                other = psum.tile([P, BANK], F32, name=f"other{first}")
-                nc.tensor.matmul(other[:], turn_matrix, trig[:, piece], start=True, stop=True)
+                swapped = psum.tile([P, BANK], F32, name=f"swapped{first}")
+                nc.tensor.matmul(swapped[:], swap_matrix, trig[:, piece], start=True, stop=True)
+                nc.vector.tensor_tensor(with_swapped[:, 1, piece], own[:, 0, piece], swapped[:], MULT)
                 nc.vector.scalar_tensor_tensor(
-                    with_other[:, 1, piece], own[:, 0, piece], sign[:, 1:2], other[:], MULT, MULT
+                    with_swapped[:, 0, piece], own[:, 1, piece], sign[:, 1:2], swapped[:], MULT, MULT
                 )
-                nc.vector.tensor_tensor(with_other[:, 0, piece], own[:, 1, piece], other[:], MULT)
 
         for w in range(2):
-            nc.vector.tensor_tensor(window[w][:].indirect(offsets[:]), with_trig[:, w, :], with_other[:, w, :], ADD)
+            nc.vector.tensor_tensor(window[w][:].indirect(offsets[:]), with_trig[:, w, :], with_swapped[:, w, :], ADD)
             for b in range(SEQUENCES):
                 nc.sync.dma_start(out_rows[:, b, (b + w) % MEMBERS, :], window_rows[w][:, b, :])

import concourse.mybir as mybir

F32 = mybir.dt.float32
U16 = mybir.dt.uint16
MULT = mybir.AluOpType.mult
ADD = mybir.AluOpType.add
NOT_EQUAL = mybir.AluOpType.not_equal
X_AXIS = mybir.AxisListType.X

P = 128
PAIRS = 64
SEQUENCES = 2
MEMBERS = 2
BANK = 512


def tile_myrotarypositionalembedding_s_kernel(tc, base, x, cosf, sinf, offs, out):
    nc = tc.nc
    slots = base.shape[1]
    tokens = x.shape[1]
    token_halves = (slice(0, tokens // 2), slice(tokens // 2, tokens))
    x_rows = x.rearrange("(b h k) t -> k b h t", b=SEQUENCES, h=MEMBERS)
    base_rows = base.rearrange("(b h k) s -> k b h s", b=SEQUENCES, h=MEMBERS)
    out_rows = out.rearrange("(b h k) s -> k b h s", b=SEQUENCES, h=MEMBERS)

    with (
        tc.tile_pool(name="held", bufs=1) as held,
        tc.psum_pool(name="psum", bufs=1) as psum,
    ):
        own = held.tile([P, MEMBERS, tokens], F32, name="own")
        trig = held.tile([P, tokens], F32, name="trig")
        offsets = held.tile([P, tokens // 16], U16, name="offsets")
        window = [held.tile([P, slots], F32, name=f"window{w}") for w in range(2)]

        own_rows = own[:].rearrange("(k b) h t -> k b h t", b=SEQUENCES)
        trig_rows = trig[:].rearrange("(k b) t -> k b t", b=SEQUENCES)
        window_rows = [window[w][:].rearrange("(k b) s -> k b s", b=SEQUENCES) for w in range(2)]

        for half in token_halves:
            nc.sync.dma_start(trig_rows[:, 0, half], cosf[0:PAIRS, half])
            nc.sync.dma_start(trig_rows[:, 1, half], sinf[PAIRS:P, half])
            for h in range(MEMBERS):
                for b in range(SEQUENCES):
                    nc.sync.dma_start(own_rows[:, b, h, half], x_rows[:, b, h, half])
        nc.sync.dma_start(offsets[:], offs)
        for w in range(2):
            for b in range(SEQUENCES):
                nc.sync.dma_start(window_rows[w][:, b, :], base_rows[:, b, (b + w) % MEMBERS, :])

        swap = held.tile([P, PAIRS, SEQUENCES], F32, name="swap")
        nc.vector.memset(swap[:], 0.0)
        nc.gpsimd.affine_select(
            out=swap[:], in_=swap[:], pattern=[[-2, PAIRS], [1, SEQUENCES]],
            compare_op=NOT_EQUAL, fill=1.0, base=-1, channel_multiplier=1,
        )
        swap_matrix = swap[:].rearrange("p k b -> p (k b)")
        is_odd = held.tile([P, 1], F32, name="is_odd")
        sign = held.tile([P, 2], F32, name="sign")
        nc.vector.reduce_sum(is_odd[:], swap[:, :, 0], axis=X_AXIS)
        nc.vector.tensor_scalar(sign[:, 0:1], is_odd[:], -2.0, 1.0, MULT, ADD)
        nc.vector.tensor_scalar(sign[:, 1:2], is_odd[:], 2.0, -1.0, MULT, ADD)

        with_trig = held.tile([P, 2, tokens], F32, name="with_trig")
        with_swapped = held.tile([P, 2, tokens], F32, name="with_swapped")
        engine_of_half = (nc.vector, nc.gpsimd)
        for number, half in enumerate(token_halves):
            engine_of_half[number].tensor_tensor(with_trig[:, 0, half], own[:, 0, half], trig[:, half], MULT)
            nc.vector.scalar_tensor_tensor(
                with_trig[:, 1, half], own[:, 1, half], sign[:, 0:1], trig[:, half], MULT, MULT
            )
            for first in range(half.start, half.stop, BANK):
                piece = slice(first, first + BANK)
                swapped = psum.tile([P, BANK], F32, name=f"swapped{first}")
                nc.tensor.matmul(swapped[:], swap_matrix, trig[:, piece], start=True, stop=True)
                nc.vector.tensor_tensor(with_swapped[:, 1, piece], own[:, 0, piece], swapped[:], MULT)
                nc.vector.scalar_tensor_tensor(
                    with_swapped[:, 0, piece], own[:, 1, piece], sign[:, 1:2], swapped[:], MULT, MULT
                )

        for w in range(2):
            nc.vector.tensor_tensor(window[w][:].indirect(offsets[:]), with_trig[:, w, :], with_swapped[:, w, :], ADD)
            for b in range(SEQUENCES):
                nc.sync.dma_start(out_rows[:, b, (b + w) % MEMBERS, :], window_rows[w][:, b, :])
